import numpy as np
import ml_dtypes

BF16 = ml_dtypes.bfloat16


def bf(x):
    return np.asarray(x, np.float32).astype(BF16)


def f32(x):
    return np.asarray(x, np.float32)


def f64(x):
    return np.asarray(x).astype(np.float64)


def striped(idx):
    return np.tile(idx.reshape(-1, 16).T, (8, 1))


D, K, N, S, W = 128, 256, 128, 256, 128
OFF = K - N
SCALE = 1.0 / np.sqrt(D)


def setup_inputs():
    return {"q": bf(np.random.standard_normal((D, N))), "k": bf(np.random.standard_normal((D, K))), "v": bf(3.0 * np.random.standard_normal((K, D))), "base": f32(0.5 * np.random.standard_normal((D, S))), "offs": striped(np.random.permutation(S)[:N])}


def reference(q, k, v, base, offs):
    idx = offs[:16].T.reshape(-1)
    sc = SCALE * (f64(k).T @ f64(q))
    t = np.arange(K)[:, None]
    i = np.arange(N)[None, :]
    seen = (t <= i + OFF) & (t > i + OFF - W)
    e = np.exp(sc) * seen
    den = e.sum(axis=0, keepdims=True)
    ctx = f64(v).T @ e
    out = f64(base).copy()
    out[:, idx] = ctx * (1.0 / den)
    return out

@@ -1,0 +1,64 @@
+import math
+
+import concourse.mybir as mybir
+
+P = 128
+D, K, N, S = 128, 256, 128, 256
+BLOCKS = K // P
+SCALE = 1.0 / math.sqrt(D)
+MASKED = -60000.0
+FLOPS = 2 * (2 * D * P * N)
+
+BF16, F32, I32, U16 = mybir.dt.bfloat16, mybir.dt.float32, mybir.dt.int32, mybir.dt.uint16
+ALU = mybir.AluOpType
+EXP = mybir.ActivationFunctionType.Exp
+
+
+def tile_attentionlayer_kernel(tc, q, k, v, base, offs, out):
+    nc = tc.nc
+    with (
+        tc.tile_pool(name="held", bufs=1) as held,
+        tc.psum_pool(name="psum", bufs=1) as psum,
+    ):
+        q_sb = held.tile([D, N], BF16, name="q_sb")
+        k_sb = held.tile([D, K], BF16, name="k_sb")
+        v_sb = held.tile([P, BLOCKS, D], BF16, name="v_sb")
+        window = held.tile([D, S], F32, name="window")
+        offsets = held.tile([P, N // 16], U16, name="offsets")
+        nc.sync.dma_start(q_sb[:], q)
+        nc.scalar.dma_start(k_sb[:], k)
+        nc.sync.dma_start(v_sb[:], v.rearrange("(b p) d -> p b d", p=P))
+        nc.scalar.dma_start(window[:], base)
+        nc.sync.dma_start(offsets[:], offs)
+
+        ahead = held.tile([P, N], I32, name="ahead")
+        nc.gpsimd.iota(ahead[:], pattern=[[1, N]], base=0, channel_multiplier=-1)
+        ident = held.tile([P, P], BF16, name="ident")
+        nc.vector.tensor_scalar(ident[:], ahead[:], 0.0, None, ALU.is_equal)
+        band_bias = held.tile([P, BLOCKS, N], BF16, name="band_bias")
+        nc.vector.tensor_scalar(band_bias[:, 0, :], ahead[:], 0.0, MASKED, ALU.is_ge, ALU.mult)
+        nc.vector.tensor_scalar(band_bias[:, 1, :], ahead[:], 0.0, MASKED, ALU.is_lt, ALU.mult)
+        ones = held.tile([P, D], BF16, name="ones")
+        nc.vector.memset(ones[:], 1.0)
+
+        sc = psum.tile([P, BLOCKS, N], F32, name="sc")
+        for b in range(BLOCKS):
+            nc.tensor.matmul(sc[:, b, :], ident[:], band_bias[:, b, :], start=True, stop=False)
+            nc.tensor.matmul(sc[:, b, :], k_sb[:, b * P : (b + 1) * P], q_sb[:], start=False, stop=True)
+
+        e = held.tile([P, BLOCKS, N], BF16, name="e")
+        nc.scalar.activation(e[:], sc[:], EXP, scale=SCALE)
+
+        den = psum.tile([D, N], F32, name="den")
+        ctx = psum.tile([D, N], F32, name="ctx")
+        for b in range(BLOCKS):
+            nc.tensor.matmul(den[:], ones[:], e[:, b, :], start=(b == 0), stop=(b == BLOCKS - 1))
+        for b in range(BLOCKS):
+            nc.tensor.matmul(ctx[:], v_sb[:, b, :], e[:, b, :], start=(b == 0), stop=(b == BLOCKS - 1))
+
+        r = held.tile([D, N], F32, name="r")
+        nc.vector.reciprocal(r[:], den[:])
+        ctx_sb = held.tile([D, N], F32, name="ctx_sb")
+        nc.scalar.copy(ctx_sb[:], ctx[:])
+        nc.vector.tensor_tensor(window[:].indirect(offsets[:]), ctx_sb[:], r[:], ALU.mult)
+        nc.sync.dma_start(out, window[:])

@@ -5,6 +5,8 @@ import concourse.mybir as mybir
 P = 128
 D, K, N, S = 128, 256, 128, 256
 BLOCKS = K // P
+CHUNKS = 2
+WIDTH = N // CHUNKS
 SCALE = 1.0 / math.sqrt(D)
 MASKED = -60000.0
 FLOPS = 2 * (2 * D * P * N)
@@ -41,23 +43,32 @@ def tile_attentionlayer_kernel(tc, q, k, v, base, offs, out):
         ones = held.tile([P, D], BF16, name="ones")
         nc.vector.memset(ones[:], 1.0)
 
-        sc = psum.tile([P, BLOCKS, N], F32, name="sc")
-        for b in range(BLOCKS):
-            nc.tensor.matmul(sc[:, b, :], ident[:], band_bias[:, b, :], start=True, stop=False)
-            nc.tensor.matmul(sc[:, b, :], k_sb[:, b * P : (b + 1) * P], q_sb[:], start=False, stop=True)
+        sc = [psum.tile([P, BLOCKS, WIDTH], F32, name=f"sc{c}") for c in range(CHUNKS)]
+        for c in range(CHUNKS):
+            nc.tensor.matmul(sc[c][:], ident[:], band_bias[:, :, c * WIDTH : (c + 1) * WIDTH], start=True, stop=False)
+        for c in range(CHUNKS):
+            for b in range(BLOCKS):
+                nc.tensor.matmul(
+                    sc[c][:, b, :],
+                    k_sb[:, b * P : (b + 1) * P],
+                    q_sb[:, c * WIDTH : (c + 1) * WIDTH],
+                    start=False,
+                    stop=(b == BLOCKS - 1),
+                )
 
         e = held.tile([P, BLOCKS, N], BF16, name="e")
-        nc.scalar.activation(e[:], sc[:], EXP, scale=SCALE)
+        den = [psum.tile([D, WIDTH], F32, name=f"den{c}") for c in range(CHUNKS)]
+        r = held.tile([D, N], F32, name="r")
+        for c in range(CHUNKS):
+            piece = slice(c * WIDTH, (c + 1) * WIDTH)
+            nc.scalar.activation(e[:, :, piece], sc[c][:], EXP, scale=SCALE)
+            for b in range(BLOCKS):
+                nc.tensor.matmul(den[c][:], ones[:], e[:, b, piece], start=(b == 0), stop=(b == BLOCKS - 1))
+            nc.vector.reciprocal(r[:, piece], den[c][:])
 
-        den = psum.tile([D, N], F32, name="den")
         ctx = psum.tile([D, N], F32, name="ctx")
         for b in range(BLOCKS):
-            nc.tensor.matmul(den[:], ones[:], e[:, b, :], start=(b == 0), stop=(b == BLOCKS - 1))
-        for b in range(BLOCKS):
             nc.tensor.matmul(ctx[:], v_sb[:, b, :], e[:, b, :], start=(b == 0), stop=(b == BLOCKS - 1))
-
-        r = held.tile([D, N], F32, name="r")
-        nc.vector.reciprocal(r[:], den[:])
         ctx_sb = held.tile([D, N], F32, name="ctx_sb")
         nc.scalar.copy(ctx_sb[:], ctx[:])
         nc.vector.tensor_tensor(window[:].indirect(offsets[:]), ctx_sb[:], r[:], ALU.mult)

@@ -5,7 +5,7 @@ import concourse.mybir as mybir
 P = 128
 D, K, N, S = 128, 256, 128, 256
 BLOCKS = K // P
-CHUNKS = 2
+CHUNKS = 4
 WIDTH = N // CHUNKS
 SCALE = 1.0 / math.sqrt(D)
 MASKED = -60000.0
@@ -43,7 +43,7 @@ def tile_attentionlayer_kernel(tc, q, k, v, base, offs, out):
         ones = held.tile([P, D], BF16, name="ones")
         nc.vector.memset(ones[:], 1.0)
 
-        sc = [psum.tile([P, BLOCKS, WIDTH], F32, name=f"sc{c}") for c in range(CHUNKS)]
+        sc = [psum.tile([P, BLOCKS, WIDTH], F32, name=f"sc{c}", tag=f"piece{c}") for c in range(CHUNKS)]
         for c in range(CHUNKS):
             nc.tensor.matmul(sc[c][:], ident[:], band_bias[:, :, c * WIDTH : (c + 1) * WIDTH], start=True, stop=False)
         for c in range(CHUNKS):
@@ -57,14 +57,14 @@ def tile_attentionlayer_kernel(tc, q, k, v, base, offs, out):
                 )
 
         e = held.tile([P, BLOCKS, N], BF16, name="e")
-        den = [psum.tile([D, WIDTH], F32, name=f"den{c}") for c in range(CHUNKS)]
         r = held.tile([D, N], F32, name="r")
         for c in range(CHUNKS):
             piece = slice(c * WIDTH, (c + 1) * WIDTH)
             nc.scalar.activation(e[:, :, piece], sc[c][:], EXP, scale=SCALE)
+            den = psum.tile([D, WIDTH], F32, name=f"den{c}", tag=f"piece{c}")
             for b in range(BLOCKS):
-                nc.tensor.matmul(den[c][:], ones[:], e[:, b, piece], start=(b == 0), stop=(b == BLOCKS - 1))
-            nc.vector.reciprocal(r[:, piece], den[c][:])
+                nc.tensor.matmul(den[:], ones[:], e[:, b, piece], start=(b == 0), stop=(b == BLOCKS - 1))
+            nc.vector.reciprocal(r[:, piece], den[:])
 
         ctx = psum.tile([D, N], F32, name="ctx")
         for b in range(BLOCKS):

@@ -5,8 +5,7 @@ import concourse.mybir as mybir
 P = 128
 D, K, N, S = 128, 256, 128, 256
 BLOCKS = K // P
-CHUNKS = 4
-WIDTH = N // CHUNKS
+PIECES = (slice(0, N // 4), slice(N // 4, N // 2), slice(N // 2, N))
 SCALE = 1.0 / math.sqrt(D)
 MASKED = -60000.0
 FLOPS = 2 * (2 * D * P * N)
@@ -43,25 +42,23 @@ def tile_attentionlayer_kernel(tc, q, k, v, base, offs, out):
         ones = held.tile([P, D], BF16, name="ones")
         nc.vector.memset(ones[:], 1.0)
 
-        sc = [psum.tile([P, BLOCKS, WIDTH], F32, name=f"sc{c}", tag=f"piece{c}") for c in range(CHUNKS)]
-        for c in range(CHUNKS):
-            nc.tensor.matmul(sc[c][:], ident[:], band_bias[:, :, c * WIDTH : (c + 1) * WIDTH], start=True, stop=False)
-        for c in range(CHUNKS):
+        sc = [
+            psum.tile([P, BLOCKS, piece.stop - piece.start], F32, name=f"sc{c}", tag=f"piece{c}")
+            for c, piece in enumerate(PIECES)
+        ]
+        for c, piece in enumerate(PIECES):
+            nc.tensor.matmul(sc[c][:], ident[:], band_bias[:, :, piece], start=True, stop=False)
+        for c, piece in enumerate(PIECES):
             for b in range(BLOCKS):
                 nc.tensor.matmul(
-                    sc[c][:, b, :],
-                    k_sb[:, b * P : (b + 1) * P],
-                    q_sb[:, c * WIDTH : (c + 1) * WIDTH],
-                    start=False,
-                    stop=(b == BLOCKS - 1),
+                    sc[c][:, b, :], k_sb[:, b * P : (b + 1) * P], q_sb[:, piece], start=False, stop=(b == BLOCKS - 1)
                 )
 
         e = held.tile([P, BLOCKS, N], BF16, name="e")
         r = held.tile([D, N], F32, name="r")
-        for c in range(CHUNKS):
-            piece = slice(c * WIDTH, (c + 1) * WIDTH)
+        for c, piece in enumerate(PIECES):
             nc.scalar.activation(e[:, :, piece], sc[c][:], EXP, scale=SCALE)
-            den = psum.tile([D, WIDTH], F32, name=f"den{c}", tag=f"piece{c}")
+            den = psum.tile([D, piece.stop - piece.start], F32, name=f"den{c}", tag=f"piece{c}")
             for b in range(BLOCKS):
                 nc.tensor.matmul(den[:], ones[:], e[:, b, piece], start=(b == 0), stop=(b == BLOCKS - 1))
             nc.vector.reciprocal(r[:, piece], den[:])

@@ -26,8 +26,8 @@ def tile_attentionlayer_kernel(tc, q, k, v, base, offs, out):
         v_sb = held.tile([P, BLOCKS, D], BF16, name="v_sb")
         window = held.tile([D, S], F32, name="window")
         offsets = held.tile([P, N // 16], U16, name="offsets")
-        nc.sync.dma_start(q_sb[:], q)
-        nc.scalar.dma_start(k_sb[:], k)
+        nc.sync.dma_start(k_sb[:], k)
+        nc.scalar.dma_start(q_sb[:], q)
         nc.sync.dma_start(v_sb[:], v.rearrange("(b p) d -> p b d", p=P))
         nc.scalar.dma_start(window[:], base)
         nc.sync.dma_start(offsets[:], offs)

@@ -8,6 +8,7 @@ BLOCKS = K // P
 PIECES = (slice(0, N // 4), slice(N // 4, N // 2), slice(N // 2, N))
 SCALE = 1.0 / math.sqrt(D)
 MASKED = -60000.0
+HALF = N // 2
 FLOPS = 2 * (2 * D * P * N)
 
 BF16, F32, I32, U16 = mybir.dt.bfloat16, mybir.dt.float32, mybir.dt.int32, mybir.dt.uint16
@@ -63,10 +64,15 @@ def tile_attentionlayer_kernel(tc, q, k, v, base, offs, out):
                 nc.tensor.matmul(den[:], ones[:], e[:, b, piece], start=(b == 0), stop=(b == BLOCKS - 1))
             nc.vector.reciprocal(r[:, piece], den[:])
 
-        ctx = psum.tile([D, N], F32, name="ctx")
-        for b in range(BLOCKS):
-            nc.tensor.matmul(ctx[:], v_sb[:, b, :], e[:, b, :], start=(b == 0), stop=(b == BLOCKS - 1))
-        ctx_sb = held.tile([D, N], F32, name="ctx_sb")
-        nc.scalar.copy(ctx_sb[:], ctx[:])
-        nc.vector.tensor_tensor(window[:].indirect(offsets[:]), ctx_sb[:], r[:], ALU.mult)
+        columns = HALF // 16
+        for h in range(2):
+            half = slice(h * HALF, (h + 1) * HALF)
+            ctx = psum.tile([D, HALF], F32, name=f"ctx{h}")
+            for b in range(BLOCKS):
+                nc.tensor.matmul(ctx[:], v_sb[:, b, :], e[:, b, half], start=(b == 0), stop=(b == BLOCKS - 1))
+            ctx_sb = held.tile([D, HALF], F32, name=f"ctx_sb{h}")
+            nc.scalar.copy(ctx_sb[:], ctx[:])
+            nc.vector.tensor_tensor(
+                window[:].indirect(offsets[:, h * columns : (h + 1) * columns]), ctx_sb[:], r[:, half], ALU.mult
+            )
         nc.sync.dma_start(out, window[:])

@@ -11,7 +11,7 @@ MASKED = -60000.0
 HALF = N // 2
 FLOPS = 2 * (2 * D * P * N)
 
-BF16, F32, I32, U16 = mybir.dt.bfloat16, mybir.dt.float32, mybir.dt.int32, mybir.dt.uint16
+BF16, F32, U16 = mybir.dt.bfloat16, mybir.dt.float32, mybir.dt.uint16
 ALU = mybir.AluOpType
 EXP = mybir.ActivationFunctionType.Exp
 
@@ -33,13 +33,21 @@ def tile_attentionlayer_kernel(tc, q, k, v, base, offs, out):
         nc.scalar.dma_start(window[:], base)
         nc.sync.dma_start(offsets[:], offs)
 
-        ahead = held.tile([P, N], I32, name="ahead")
-        nc.gpsimd.iota(ahead[:], pattern=[[1, N]], base=0, channel_multiplier=-1)
+        one = held.tile([P, 1], F32, name="one")
+        nc.vector.memset(one[:], 1.0)
+        column = held.tile([P, N], BF16, name="column")
+        nc.vector.tensor_tensor_scan(
+            column[:], one[:].to_broadcast([P, N]), one[:].to_broadcast([P, N]), -1.0, ALU.mult, ALU.add
+        )
+        share = held.tile([P, 1], BF16, name="share")
+        nc.vector.memset(share[:], 1.0 / P)
+        partition = psum.tile([P, 1], F32, name="partition")
+        nc.tensor.matmul(partition[:], column[:], share[:], start=True, stop=True)
         ident = held.tile([P, P], BF16, name="ident")
-        nc.vector.tensor_scalar(ident[:], ahead[:], 0.0, None, ALU.is_equal)
+        nc.vector.tensor_scalar(ident[:], column[:], partition[:], None, ALU.is_equal)
         band_bias = held.tile([P, BLOCKS, N], BF16, name="band_bias")
-        nc.vector.tensor_scalar(band_bias[:, 0, :], ahead[:], 0.0, MASKED, ALU.is_ge, ALU.mult)
-        nc.vector.tensor_scalar(band_bias[:, 1, :], ahead[:], 0.0, MASKED, ALU.is_lt, ALU.mult)
+        nc.vector.tensor_scalar(band_bias[:, 0, :], column[:], partition[:], MASKED, ALU.is_ge, ALU.mult)
+        nc.vector.tensor_scalar(band_bias[:, 1, :], column[:], partition[:], MASKED, ALU.is_lt, ALU.mult)
         ones = held.tile([P, D], BF16, name="ones")
         nc.vector.memset(ones[:], 1.0)
 

import math

import concourse.mybir as mybir

P = 128
D, K, N, S = 128, 256, 128, 256
BLOCKS = K // P
PIECES = (slice(0, N // 4), slice(N // 4, N // 2), slice(N // 2, N))
SCALE = 1.0 / math.sqrt(D)
MASKED = -60000.0
HALF = N // 2
FLOPS = 2 * (2 * D * P * N)

BF16, F32, U16 = mybir.dt.bfloat16, mybir.dt.float32, mybir.dt.uint16
ALU = mybir.AluOpType
EXP = mybir.ActivationFunctionType.Exp


def tile_attentionlayer_kernel(tc, q, k, v, base, offs, out):
    nc = tc.nc
    with (
        tc.tile_pool(name="held", bufs=1) as held,
        tc.psum_pool(name="psum", bufs=1) as psum,
    ):
        q_sb = held.tile([D, N], BF16, name="q_sb")
        k_sb = held.tile([D, K], BF16, name="k_sb")
        v_sb = held.tile([P, BLOCKS, D], BF16, name="v_sb")
        window = held.tile([D, S], F32, name="window")
        offsets = held.tile([P, N // 16], U16, name="offsets")
        nc.sync.dma_start(k_sb[:], k)
        nc.scalar.dma_start(q_sb[:], q)
        nc.sync.dma_start(v_sb[:], v.rearrange("(b p) d -> p b d", p=P))
        nc.scalar.dma_start(window[:], base)
        nc.sync.dma_start(offsets[:], offs)

        one = held.tile([P, 1], F32, name="one")
        nc.vector.memset(one[:], 1.0)
        column = held.tile([P, N], BF16, name="column")
        nc.vector.tensor_tensor_scan(
            column[:], one[:].to_broadcast([P, N]), one[:].to_broadcast([P, N]), -1.0, ALU.mult, ALU.add
        )
        share = held.tile([P, 1], BF16, name="share")
        nc.vector.memset(share[:], 1.0 / P)
        partition = psum.tile([P, 1], F32, name="partition")
        nc.tensor.matmul(partition[:], column[:], share[:], start=True, stop=True)
        ident = held.tile([P, P], BF16, name="ident")
        nc.vector.tensor_scalar(ident[:], column[:], partition[:], None, ALU.is_equal)
        band_bias = held.tile([P, BLOCKS, N], BF16, name="band_bias")
        nc.vector.tensor_scalar(band_bias[:, 0, :], column[:], partition[:], MASKED, ALU.is_ge, ALU.mult)
        nc.vector.tensor_scalar(band_bias[:, 1, :], column[:], partition[:], MASKED, ALU.is_lt, ALU.mult)
        ones = held.tile([P, D], BF16, name="ones")
        nc.vector.memset(ones[:], 1.0)

        sc = [
            psum.tile([P, BLOCKS, piece.stop - piece.start], F32, name=f"sc{c}", tag=f"piece{c}")
            for c, piece in enumerate(PIECES)
        ]
        for c, piece in enumerate(PIECES):
            nc.tensor.matmul(sc[c][:], ident[:], band_bias[:, :, piece], start=True, stop=False)
        for c, piece in enumerate(PIECES):
            for b in range(BLOCKS):
                nc.tensor.matmul(
                    sc[c][:, b, :], k_sb[:, b * P : (b + 1) * P], q_sb[:, piece], start=False, stop=(b == BLOCKS - 1)
                )

        e = held.tile([P, BLOCKS, N], BF16, name="e")
        r = held.tile([D, N], F32, name="r")
        for c, piece in enumerate(PIECES):
            nc.scalar.activation(e[:, :, piece], sc[c][:], EXP, scale=SCALE)
            den = psum.tile([D, piece.stop - piece.start], F32, name=f"den{c}", tag=f"piece{c}")
            for b in range(BLOCKS):
                nc.tensor.matmul(den[:], ones[:], e[:, b, piece], start=(b == 0), stop=(b == BLOCKS - 1))
            nc.vector.reciprocal(r[:, piece], den[:])

        columns = HALF // 16
        for h in range(2):
            half = slice(h * HALF, (h + 1) * HALF)
            ctx = psum.tile([D, HALF], F32, name=f"ctx{h}")
            for b in range(BLOCKS):
                nc.tensor.matmul(ctx[:], v_sb[:, b, :], e[:, b, half], start=(b == 0), stop=(b == BLOCKS - 1))
            ctx_sb = held.tile([D, HALF], F32, name=f"ctx_sb{h}")
            nc.scalar.copy(ctx_sb[:], ctx[:])
            nc.vector.tensor_tensor(
                window[:].indirect(offsets[:, h * columns : (h + 1) * columns]), ctx_sb[:], r[:, half], ALU.mult
            )
        nc.sync.dma_start(out, window[:])
